import numpy as np
import ml_dtypes


def mxq(x, axis, fmt="e4m3"):
    dtype, down = {"e4m3": (ml_dtypes.float8_e4m3fn, 7), "e5m2": (ml_dtypes.float8_e5m2, 14)}[fmt]
    v = np.moveaxis(np.asarray(x, np.float32).astype(ml_dtypes.bfloat16).astype(np.float64), axis, -1)
    blocks = v.reshape(v.shape[:-1] + (-1, 32))
    amax = np.abs(blocks).max(-1, keepdims=True)
    byte = np.maximum(np.where(amax > 0, np.frexp(amax)[1] - 1 + 127, 0) - down, 1)
    scale = np.exp2(byte - 127.0)
    codes = (blocks / scale).astype(np.float32).astype(dtype).astype(np.float64)
    return np.moveaxis((codes * scale).reshape(v.shape), -1, axis)


WIDE = False


def mx_kscale(k):
    if not WIDE:
        return np.ones(k)
    levels = np.array([10, -10, 5, -5, 0])
    a = np.random.permutation(np.resize(levels, k // 512 * 4)).reshape(k // 512, 4)
    idx = np.arange(k)
    return np.exp2(a[idx // 512, idx % 128 // 32])


BF16 = ml_dtypes.bfloat16


def bf(x):
    return np.asarray(x, np.float32).astype(BF16)


def f64(x):
    return np.asarray(x).astype(np.float64)


B, S, IN, OUT, A, R = 8, 128, 1024, 128, 8, 128
G = B // A
SCALING = 2.0


def setup_inputs():
    s = mx_kscale(IN)
    return {"data": bf(np.random.standard_normal((B, S, IN)) * s),
            "W": bf(np.random.standard_normal((OUT, IN)) / np.sqrt(IN) / s),
            "t_lora": bf(np.random.standard_normal((A, G, S, R))),
            "lora_b": bf(np.random.standard_normal((A, OUT, R)) * 0.5 / np.sqrt(R))}


def reference(data, W, t_lora, lora_b):
    base = mxq(f64(data), 2, "e4m3") @ mxq(f64(W), 1, "e4m3").T
    delta = (f64(t_lora).reshape(A, G * S, R) @ f64(lora_b).transpose(0, 2, 1)) * SCALING
    return base + delta.reshape(B, S, OUT)

@@ -1,0 +1,113 @@
+from contextlib import ExitStack
+
+import concourse.mybir as mybir
+from concourse.masks import make_identity
+
+BF16 = mybir.dt.bfloat16
+F32 = mybir.dt.float32
+U32 = mybir.dt.uint32
+U8 = mybir.dt.uint8
+FP8X4 = mybir.dt.float8_e4m3fn_x4
+
+P = 128
+B, S, IN, OUT, R = 8, 128, 1024, 128, 128
+SCALING = 2.0
+
+PACK = 4
+K_PASS = P * PACK
+PASSES = IN // K_PASS
+PAIR = 2
+WORD_BLOCKS = IN // (PAIR * P)
+BLOCKS_PER_PASS = WORD_BLOCKS // PASSES
+ADAPTERS_PER_BANK = 4
+
+FLOPS = 2 * B * S * IN * OUT + 2 * B * S * R * OUT
+
+
+def quantise_rows(nc, psum, stage, ident_f32, rows, codes, scales):
+    words = rows.bitcast(F32)
+    flipped = psum.tile([P, WORD_BLOCKS, P], F32, tag="bank")
+    for j in range(WORD_BLOCKS):
+        nc.tensor.transpose(flipped[:, j, :], words[:, j * P : (j + 1) * P], ident_f32[:])
+    grouped = stage.tile([P, PASSES * P * PACK], BF16, align_bytes=64)
+    nc.scalar.copy(
+        out=grouped[:].bitcast(F32).rearrange("p (g r u) -> p g r u", g=PASSES, u=BLOCKS_PER_PASS),
+        in_=flipped[:].rearrange("p (g u) r -> p g r u", u=BLOCKS_PER_PASS),
+    )
+    nc.vector.quantize_mx(out=codes.bitcast(FP8X4), scales=scales, in_=grouped[:])
+
+
+def tile_linear_pa_s_kernel(tc, data, W, t_lora, lora_b, out):
+    nc = tc.nc
+    with ExitStack() as ctx:
+        keep = ctx.enter_context(tc.tile_pool(name="keep", bufs=1))
+        stage = ctx.enter_context(tc.tile_pool(name="stage", bufs=3))
+        psum = ctx.enter_context(tc.psum_pool(name="psum", bufs=8))
+
+        ident_f32 = keep.tile([P, P], F32)
+        make_identity(nc, ident_f32[:])
+        ident_bf16 = keep.tile([P, P], BF16)
+        make_identity(nc, ident_bf16[:])
+
+        t_sb = keep.tile([P, B, R], BF16)
+        nc.sync.dma_start(out=t_sb[:], in_=t_lora.rearrange("a g s r -> s (a g) r"))
+        b_sb = keep.tile([P, B, R], BF16)
+        nc.sync.dma_start(out=b_sb[:], in_=lora_b.rearrange("a o r -> o a r"))
+        w_sb = keep.tile([P, IN], BF16)
+        nc.sync.dma_start(out=w_sb[:], in_=W[:, :])
+        x_sb = keep.tile([P, B, IN], BF16)
+        for b in range(B):
+            nc.sync.dma_start(out=x_sb[:, b, :], in_=data[b, :, :])
+
+        tT_ps = psum.tile([P, B, S], BF16, tag="bank")
+        for a in range(B):
+            nc.tensor.transpose(tT_ps[:, a, :], t_sb[:, a, :], ident_bf16[:])
+        tT = keep.tile([P, B, S], BF16)
+        nc.vector.tensor_copy(out=tT[:], in_=tT_ps[:])
+        bT_ps = psum.tile([P, B, OUT], BF16, tag="bank")
+        for a in range(B):
+            nc.tensor.transpose(bT_ps[:, a, :], b_sb[:, a, :], ident_bf16[:])
+        bT = keep.tile([P, B, OUT], BF16)
+        nc.scalar.copy(out=bT[:], in_=bT_ps[:])
+
+        delta = keep.tile([P, B, OUT], F32)
+        for first in range(0, B, ADAPTERS_PER_BANK):
+            delta_ps = psum.tile([P, ADAPTERS_PER_BANK, OUT], F32, tag="bank")
+            for i in range(ADAPTERS_PER_BANK):
+                a = first + i
+                nc.tensor.matmul(
+                    delta_ps[:, i, :], lhsT=tT[:, a, :], rhs=bT[:, a, :], start=True, stop=True
+                )
+            nc.vector.tensor_copy(out=delta[:, first : first + ADAPTERS_PER_BANK, :], in_=delta_ps[:])
+
+        w_codes = keep.tile([P, PASSES * OUT], U32, align_bytes=64)
+        w_scales = keep.tile([P, PASSES * OUT], U8, align_bytes=64)
+        quantise_rows(nc, psum, stage, ident_f32, w_sb[:], w_codes[:], w_scales[:])
+
+        x_codes = keep.tile([P, B, PASSES * S], U32, align_bytes=64)
+        x_scales = keep.tile([P, B, PASSES * S], U8, align_bytes=64)
+        result = keep.tile([P, B, OUT], F32)
+        for b in range(B):
+            quantise_rows(
+                nc, psum, stage, ident_f32, x_sb[:, b, :], x_codes[:, b, :], x_scales[:, b, :]
+            )
+            acc = psum.tile([P, OUT], F32, tag="bank")
+            for g in range(PASSES):
+                nc.tensor.matmul_mx(
+                    out=acc[:],
+                    lhsT=x_codes[:, b, g * S : (g + 1) * S].bitcast(FP8X4),
+                    lhsT_scale=x_scales[:, b, g * S : (g + 1) * S],
+                    rhs=w_codes[:, g * OUT : (g + 1) * OUT].bitcast(FP8X4),
+                    rhs_scale=w_scales[:, g * OUT : (g + 1) * OUT],
+                    start=(g == 0),
+                    stop=(g == PASSES - 1),
+                )
+            nc.vector.scalar_tensor_tensor(
+                out=result[:, b, :],
+                in0=delta[:, b, :],
+                scalar=SCALING,
+                in1=acc[:],
+                op0=mybir.AluOpType.mult,
+                op1=mybir.AluOpType.add,
+            )
+            nc.sync.dma_start(out=out[b, :, :], in_=result[:, b, :])

@@ -20,6 +20,7 @@ PAIR = 2
 WORD_BLOCKS = IN // (PAIR * P)
 BLOCKS_PER_PASS = WORD_BLOCKS // PASSES
 ADAPTERS_PER_BANK = 4
+LEAD = 3
 
 FLOPS = 2 * B * S * IN * OUT + 2 * B * S * R * OUT
 
@@ -41,7 +42,7 @@ def tile_linear_pa_s_kernel(tc, data, W, t_lora, lora_b, out):
     nc = tc.nc
     with ExitStack() as ctx:
         keep = ctx.enter_context(tc.tile_pool(name="keep", bufs=1))
-        stage = ctx.enter_context(tc.tile_pool(name="stage", bufs=3))
+        stage = ctx.enter_context(tc.tile_pool(name="stage", bufs=LEAD + 1))
         psum = ctx.enter_context(tc.psum_pool(name="psum", bufs=8))
 
         ident_f32 = keep.tile([P, P], F32)
@@ -59,38 +60,21 @@ def tile_linear_pa_s_kernel(tc, data, W, t_lora, lora_b, out):
         for b in range(B):
             nc.sync.dma_start(out=x_sb[:, b, :], in_=data[b, :, :])
 
-        tT_ps = psum.tile([P, B, S], BF16, tag="bank")
-        for a in range(B):
-            nc.tensor.transpose(tT_ps[:, a, :], t_sb[:, a, :], ident_bf16[:])
-        tT = keep.tile([P, B, S], BF16)
-        nc.vector.tensor_copy(out=tT[:], in_=tT_ps[:])
-        bT_ps = psum.tile([P, B, OUT], BF16, tag="bank")
-        for a in range(B):
-            nc.tensor.transpose(bT_ps[:, a, :], b_sb[:, a, :], ident_bf16[:])
-        bT = keep.tile([P, B, OUT], BF16)
-        nc.scalar.copy(out=bT[:], in_=bT_ps[:])
-
-        delta = keep.tile([P, B, OUT], F32)
-        for first in range(0, B, ADAPTERS_PER_BANK):
-            delta_ps = psum.tile([P, ADAPTERS_PER_BANK, OUT], F32, tag="bank")
-            for i in range(ADAPTERS_PER_BANK):
-                a = first + i
-                nc.tensor.matmul(
-                    delta_ps[:, i, :], lhsT=tT[:, a, :], rhs=bT[:, a, :], start=True, stop=True
-                )
-            nc.vector.tensor_copy(out=delta[:, first : first + ADAPTERS_PER_BANK, :], in_=delta_ps[:])
-
         w_codes = keep.tile([P, PASSES * OUT], U32, align_bytes=64)
         w_scales = keep.tile([P, PASSES * OUT], U8, align_bytes=64)
-        quantise_rows(nc, psum, stage, ident_f32, w_sb[:], w_codes[:], w_scales[:])
-
         x_codes = keep.tile([P, B, PASSES * S], U32, align_bytes=64)
         x_scales = keep.tile([P, B, PASSES * S], U8, align_bytes=64)
+        tT = keep.tile([P, B, S], BF16)
+        bT = keep.tile([P, B, OUT], BF16)
+        delta = keep.tile([P, B, OUT], F32)
         result = keep.tile([P, B, OUT], F32)
-        for b in range(B):
+
+        def quantise_batch_row(b):
             quantise_rows(
                 nc, psum, stage, ident_f32, x_sb[:, b, :], x_codes[:, b, :], x_scales[:, b, :]
             )
+
+        def multiply_batch_row(b):
             acc = psum.tile([P, OUT], F32, tag="bank")
             for g in range(PASSES):
                 nc.tensor.matmul_mx(
@@ -111,3 +95,33 @@ def tile_linear_pa_s_kernel(tc, data, W, t_lora, lora_b, out):
                 op1=mybir.AluOpType.add,
             )
             nc.sync.dma_start(out=out[b, :, :], in_=result[:, b, :])
+
+        with tc.manual_schedule():
+            tT_ps = psum.tile([P, B, S], BF16, tag="bank")
+            for a in range(B):
+                nc.tensor.transpose(tT_ps[:, a, :], t_sb[:, a, :], ident_bf16[:])
+            nc.vector.tensor_copy(out=tT[:], in_=tT_ps[:])
+            bT_ps = psum.tile([P, B, OUT], BF16, tag="bank")
+            for a in range(B):
+                nc.tensor.transpose(bT_ps[:, a, :], b_sb[:, a, :], ident_bf16[:])
+            nc.scalar.copy(out=bT[:], in_=bT_ps[:])
+
+            quantise_rows(nc, psum, stage, ident_f32, w_sb[:], w_codes[:], w_scales[:])
+            quantise_batch_row(0)
+
+            for first in range(0, B, ADAPTERS_PER_BANK):
+                delta_ps = psum.tile([P, ADAPTERS_PER_BANK, OUT], F32, tag="bank")
+                for i in range(ADAPTERS_PER_BANK):
+                    a = first + i
+                    nc.tensor.matmul(
+                        delta_ps[:, i, :], lhsT=tT[:, a, :], rhs=bT[:, a, :], start=True, stop=True
+                    )
+                nc.vector.tensor_copy(
+                    out=delta[:, first : first + ADAPTERS_PER_BANK, :], in_=delta_ps[:]
+                )
+
+            for b in range(1, B + LEAD):
+                if b < B:
+                    quantise_batch_row(b)
+                if b >= LEAD:
+                    multiply_batch_row(b - LEAD)

@@ -20,7 +20,9 @@ PAIR = 2
 WORD_BLOCKS = IN // (PAIR * P)
 BLOCKS_PER_PASS = WORD_BLOCKS // PASSES
 ADAPTERS_PER_BANK = 4
-LEAD = 3
+ROUND = 2
+ROUNDS = B // ROUND
+LEAD = 2
 
 FLOPS = 2 * B * S * IN * OUT + 2 * B * S * R * OUT
 
@@ -42,7 +44,7 @@ def tile_linear_pa_s_kernel(tc, data, W, t_lora, lora_b, out):
     nc = tc.nc
     with ExitStack() as ctx:
         keep = ctx.enter_context(tc.tile_pool(name="keep", bufs=1))
-        stage = ctx.enter_context(tc.tile_pool(name="stage", bufs=LEAD + 1))
+        stage = ctx.enter_context(tc.tile_pool(name="stage", bufs=(LEAD + 1) * ROUND))
         psum = ctx.enter_context(tc.psum_pool(name="psum", bufs=8))
 
         ident_f32 = keep.tile([P, P], F32)
@@ -50,78 +52,84 @@ def tile_linear_pa_s_kernel(tc, data, W, t_lora, lora_b, out):
         ident_bf16 = keep.tile([P, P], BF16)
         make_identity(nc, ident_bf16[:])
 
-        t_sb = keep.tile([P, B, R], BF16)
-        nc.sync.dma_start(out=t_sb[:], in_=t_lora.rearrange("a g s r -> s (a g) r"))
-        b_sb = keep.tile([P, B, R], BF16)
-        nc.sync.dma_start(out=b_sb[:], in_=lora_b.rearrange("a o r -> o a r"))
         w_sb = keep.tile([P, IN], BF16)
         nc.sync.dma_start(out=w_sb[:], in_=W[:, :])
         x_sb = keep.tile([P, B, IN], BF16)
         for b in range(B):
             nc.sync.dma_start(out=x_sb[:, b, :], in_=data[b, :, :])
+        t_sb = keep.tile([P, B, R], BF16)
+        b_sb = keep.tile([P, B, R], BF16)
+        for first in range(0, B, ADAPTERS_PER_BANK):
+            these = slice(first, first + ADAPTERS_PER_BANK)
+            nc.sync.dma_start(
+                out=t_sb[:, these, :], in_=t_lora[these].rearrange("a g s r -> s (a g) r")
+            )
+            nc.sync.dma_start(out=b_sb[:, these, :], in_=lora_b[these].rearrange("a o r -> o a r"))
 
         w_codes = keep.tile([P, PASSES * OUT], U32, align_bytes=64)
         w_scales = keep.tile([P, PASSES * OUT], U8, align_bytes=64)
         x_codes = keep.tile([P, B, PASSES * S], U32, align_bytes=64)
         x_scales = keep.tile([P, B, PASSES * S], U8, align_bytes=64)
-        tT = keep.tile([P, B, S], BF16)
-        bT = keep.tile([P, B, OUT], BF16)
-        delta = keep.tile([P, B, OUT], F32)
+        base = keep.tile([P, B, OUT], F32)
+        tbT = keep.tile([P, B, 2, P], BF16)
         result = keep.tile([P, B, OUT], F32)
 
-        def quantise_batch_row(b):
-            quantise_rows(
-                nc, psum, stage, ident_f32, x_sb[:, b, :], x_codes[:, b, :], x_scales[:, b, :]
-            )
+        def quantise_round(first):
+            for b in range(first, first + ROUND):
+                quantise_rows(
+                    nc, psum, stage, ident_f32, x_sb[:, b, :], x_codes[:, b, :], x_scales[:, b, :]
+                )
 
-        def multiply_batch_row(b):
-            acc = psum.tile([P, OUT], F32, tag="bank")
-            for g in range(PASSES):
-                nc.tensor.matmul_mx(
-                    out=acc[:],
-                    lhsT=x_codes[:, b, g * S : (g + 1) * S].bitcast(FP8X4),
-                    lhsT_scale=x_scales[:, b, g * S : (g + 1) * S],
-                    rhs=w_codes[:, g * OUT : (g + 1) * OUT].bitcast(FP8X4),
-                    rhs_scale=w_scales[:, g * OUT : (g + 1) * OUT],
-                    start=(g == 0),
-                    stop=(g == PASSES - 1),
+        def multiply_round(first):
+            acc = psum.tile([P, ROUND, OUT], F32, tag="bank")
+            for i in range(ROUND):
+                b = first + i
+                for g in range(PASSES):
+                    nc.tensor.matmul_mx(
+                        out=acc[:, i, :],
+                        lhsT=x_codes[:, b, g * S : (g + 1) * S].bitcast(FP8X4),
+                        lhsT_scale=x_scales[:, b, g * S : (g + 1) * S],
+                        rhs=w_codes[:, g * OUT : (g + 1) * OUT].bitcast(FP8X4),
+                        rhs_scale=w_scales[:, g * OUT : (g + 1) * OUT],
+                        start=(g == 0),
+                        stop=(g == PASSES - 1),
+                    )
+            nc.vector.tensor_copy(out=base[:, first : first + ROUND, :], in_=acc[:])
+
+        def flip_adapters(first):
+            tbT_ps = psum.tile([P, ROUND, 2, P], BF16, tag="bank")
+            for i in range(ROUND):
+                nc.tensor.transpose(tbT_ps[:, i, 0, :], t_sb[:, first + i, :], ident_bf16[:])
+                nc.tensor.transpose(tbT_ps[:, i, 1, :], b_sb[:, first + i, :], ident_bf16[:])
+            nc.scalar.copy(out=tbT[:, first : first + ROUND, :, :], in_=tbT_ps[:])
+
+        def add_adapters(first):
+            these = slice(first, first + ROUND)
+            delta_ps = psum.tile([P, ROUND, OUT], F32, tag="bank")
+            for i in range(ROUND):
+                nc.tensor.matmul(
+                    delta_ps[:, i, :],
+                    lhsT=tbT[:, first + i, 0, :],
+                    rhs=tbT[:, first + i, 1, :],
+                    start=True,
+                    stop=True,
                 )
             nc.vector.scalar_tensor_tensor(
-                out=result[:, b, :],
-                in0=delta[:, b, :],
+                out=result[:, these, :],
+                in0=delta_ps[:],
                 scalar=SCALING,
-                in1=acc[:],
+                in1=base[:, these, :],
                 op0=mybir.AluOpType.mult,
                 op1=mybir.AluOpType.add,
             )
-            nc.sync.dma_start(out=out[b, :, :], in_=result[:, b, :])
+            nc.sync.dma_start(out=out[these].rearrange("b s o -> s b o"), in_=result[:, these, :])
 
+        starts = [quantise_round] * ROUNDS + [flip_adapters] * ROUNDS
+        finishes = [multiply_round] * ROUNDS + [add_adapters] * ROUNDS
         with tc.manual_schedule():
-            tT_ps = psum.tile([P, B, S], BF16, tag="bank")
-            for a in range(B):
-                nc.tensor.transpose(tT_ps[:, a, :], t_sb[:, a, :], ident_bf16[:])
-            nc.vector.tensor_copy(out=tT[:], in_=tT_ps[:])
-            bT_ps = psum.tile([P, B, OUT], BF16, tag="bank")
-            for a in range(B):
-                nc.tensor.transpose(bT_ps[:, a, :], b_sb[:, a, :], ident_bf16[:])
-            nc.scalar.copy(out=bT[:], in_=bT_ps[:])
-
             quantise_rows(nc, psum, stage, ident_f32, w_sb[:], w_codes[:], w_scales[:])
-            quantise_batch_row(0)
-
-            for first in range(0, B, ADAPTERS_PER_BANK):
-                delta_ps = psum.tile([P, ADAPTERS_PER_BANK, OUT], F32, tag="bank")
-                for i in range(ADAPTERS_PER_BANK):
-                    a = first + i
-                    nc.tensor.matmul(
-                        delta_ps[:, i, :], lhsT=tT[:, a, :], rhs=bT[:, a, :], start=True, stop=True
-                    )
-                nc.vector.tensor_copy(
-                    out=delta[:, first : first + ADAPTERS_PER_BANK, :], in_=delta_ps[:]
-                )
-
-            for b in range(1, B + LEAD):
-                if b < B:
-                    quantise_batch_row(b)
-                if b >= LEAD:
-                    multiply_batch_row(b - LEAD)
+            for step in range(2 * ROUNDS + LEAD):
+                if step < 2 * ROUNDS:
+                    starts[step]((step % ROUNDS) * ROUND)
+                if step >= LEAD:
+                    finishes[step - LEAD](((step - LEAD) % ROUNDS) * ROUND)

@@ -23,6 +23,7 @@ ADAPTERS_PER_BANK = 4
 ROUND = 2
 ROUNDS = B // ROUND
 LEAD = 2
+WARM_PASSES = 16
 
 FLOPS = 2 * B * S * IN * OUT + 2 * B * S * R * OUT
 
@@ -124,12 +125,33 @@ def tile_linear_pa_s_kernel(tc, data, W, t_lora, lora_b, out):
             )
             nc.sync.dma_start(out=out[these].rearrange("b s o -> s b o"), in_=result[:, these, :])
 
-        starts = [quantise_round] * ROUNDS + [flip_adapters] * ROUNDS
-        finishes = [multiply_round] * ROUNDS + [add_adapters] * ROUNDS
         with tc.manual_schedule():
+            zeros = keep.tile([P, P * PACK], BF16, align_bytes=64)
+            nc.vector.memset(zeros[:], 0.0)
+            zero_codes = keep.tile([P, P], U32, align_bytes=64)
+            zero_scales = keep.tile([P, P], U8, align_bytes=64)
+            nc.vector.quantize_mx(
+                out=zero_codes[:].bitcast(FP8X4), scales=zero_scales[:], in_=zeros[:]
+            )
+            warm_ps = psum.tile([P, P], F32, tag="bank")
+            for i in range(WARM_PASSES):
+                nc.tensor.matmul_mx(
+                    out=warm_ps[:],
+                    lhsT=zero_codes[:].bitcast(FP8X4),
+                    lhsT_scale=zero_scales[:],
+                    rhs=zero_codes[:].bitcast(FP8X4),
+                    rhs_scale=zero_scales[:],
+                    start=True,
+                    stop=True,
+                )
             quantise_rows(nc, psum, stage, ident_f32, w_sb[:], w_codes[:], w_scales[:])
             for step in range(2 * ROUNDS + LEAD):
-                if step < 2 * ROUNDS:
-                    starts[step]((step % ROUNDS) * ROUND)
-                if step >= LEAD:
-                    finishes[step - LEAD](((step - LEAD) % ROUNDS) * ROUND)
+                if step < ROUNDS:
+                    quantise_round(step * ROUND)
+                elif step < 2 * ROUNDS:
+                    flip_adapters((step - ROUNDS) * ROUND)
+                due = step - LEAD
+                if 0 <= due < ROUNDS:
+                    multiply_round(due * ROUND)
+                elif due >= ROUNDS:
+                    add_adapters((due - ROUNDS) * ROUND)

@@ -23,7 +23,7 @@ ADAPTERS_PER_BANK = 4
 ROUND = 2
 ROUNDS = B // ROUND
 LEAD = 2
-WARM_PASSES = 16
+WARM_PASSES = 8
 
 FLOPS = 2 * B * S * IN * OUT + 2 * B * S * R * OUT
 
@@ -133,17 +133,21 @@ def tile_linear_pa_s_kernel(tc, data, W, t_lora, lora_b, out):
             nc.vector.quantize_mx(
                 out=zero_codes[:].bitcast(FP8X4), scales=zero_scales[:], in_=zeros[:]
             )
-            warm_ps = psum.tile([P, P], F32, tag="bank")
-            for i in range(WARM_PASSES):
-                nc.tensor.matmul_mx(
-                    out=warm_ps[:],
-                    lhsT=zero_codes[:].bitcast(FP8X4),
-                    lhsT_scale=zero_scales[:],
-                    rhs=zero_codes[:].bitcast(FP8X4),
-                    rhs_scale=zero_scales[:],
-                    start=True,
-                    stop=True,
-                )
+
+            def spin():
+                warm_ps = psum.tile([P, P], F32, tag="bank")
+                for i in range(WARM_PASSES):
+                    nc.tensor.matmul_mx(
+                        out=warm_ps[:],
+                        lhsT=zero_codes[:].bitcast(FP8X4),
+                        lhsT_scale=zero_scales[:],
+                        rhs=zero_codes[:].bitcast(FP8X4),
+                        rhs_scale=zero_scales[:],
+                        start=True,
+                        stop=True,
+                    )
+
+            spin()
             quantise_rows(nc, psum, stage, ident_f32, w_sb[:], w_codes[:], w_scales[:])
             for step in range(2 * ROUNDS + LEAD):
                 if step < ROUNDS:
@@ -151,7 +155,9 @@ def tile_linear_pa_s_kernel(tc, data, W, t_lora, lora_b, out):
                 elif step < 2 * ROUNDS:
                     flip_adapters((step - ROUNDS) * ROUND)
                 due = step - LEAD
-                if 0 <= due < ROUNDS:
+                if due < 0:
+                    spin()
+                elif due < ROUNDS:
                     multiply_round(due * ROUND)
                 elif due >= ROUNDS:
                     add_adapters((due - ROUNDS) * ROUND)

from contextlib import ExitStack

import concourse.mybir as mybir
from concourse.masks import make_identity

BF16 = mybir.dt.bfloat16
F32 = mybir.dt.float32
U32 = mybir.dt.uint32
U8 = mybir.dt.uint8
FP8X4 = mybir.dt.float8_e4m3fn_x4

P = 128
B, S, IN, OUT, R = 8, 128, 1024, 128, 128
SCALING = 2.0

PACK = 4
K_PASS = P * PACK
PASSES = IN // K_PASS
PAIR = 2
WORD_BLOCKS = IN // (PAIR * P)
BLOCKS_PER_PASS = WORD_BLOCKS // PASSES
ADAPTERS_PER_BANK = 4
ROUND = 2
ROUNDS = B // ROUND
LEAD = 2
WARM_PASSES = 8

FLOPS = 2 * B * S * IN * OUT + 2 * B * S * R * OUT


def quantise_rows(nc, psum, stage, ident_f32, rows, codes, scales):
    words = rows.bitcast(F32)
    flipped = psum.tile([P, WORD_BLOCKS, P], F32, tag="bank")
    for j in range(WORD_BLOCKS):
        nc.tensor.transpose(flipped[:, j, :], words[:, j * P : (j + 1) * P], ident_f32[:])
    grouped = stage.tile([P, PASSES * P * PACK], BF16, align_bytes=64)
    nc.scalar.copy(
        out=grouped[:].bitcast(F32).rearrange("p (g r u) -> p g r u", g=PASSES, u=BLOCKS_PER_PASS),
        in_=flipped[:].rearrange("p (g u) r -> p g r u", u=BLOCKS_PER_PASS),
    )
    nc.vector.quantize_mx(out=codes.bitcast(FP8X4), scales=scales, in_=grouped[:])


def tile_linear_pa_s_kernel(tc, data, W, t_lora, lora_b, out):
    nc = tc.nc
    with ExitStack() as ctx:
        keep = ctx.enter_context(tc.tile_pool(name="keep", bufs=1))
        stage = ctx.enter_context(tc.tile_pool(name="stage", bufs=(LEAD + 1) * ROUND))
        psum = ctx.enter_context(tc.psum_pool(name="psum", bufs=8))

        ident_f32 = keep.tile([P, P], F32)
        make_identity(nc, ident_f32[:])
        ident_bf16 = keep.tile([P, P], BF16)
        make_identity(nc, ident_bf16[:])

        w_sb = keep.tile([P, IN], BF16)
        nc.sync.dma_start(out=w_sb[:], in_=W[:, :])
        x_sb = keep.tile([P, B, IN], BF16)
        for b in range(B):
            nc.sync.dma_start(out=x_sb[:, b, :], in_=data[b, :, :])
        t_sb = keep.tile([P, B, R], BF16)
        b_sb = keep.tile([P, B, R], BF16)
        for first in range(0, B, ADAPTERS_PER_BANK):
            these = slice(first, first + ADAPTERS_PER_BANK)
            nc.sync.dma_start(
                out=t_sb[:, these, :], in_=t_lora[these].rearrange("a g s r -> s (a g) r")
            )
            nc.sync.dma_start(out=b_sb[:, these, :], in_=lora_b[these].rearrange("a o r -> o a r"))

        w_codes = keep.tile([P, PASSES * OUT], U32, align_bytes=64)
        w_scales = keep.tile([P, PASSES * OUT], U8, align_bytes=64)
        x_codes = keep.tile([P, B, PASSES * S], U32, align_bytes=64)
        x_scales = keep.tile([P, B, PASSES * S], U8, align_bytes=64)
        base = keep.tile([P, B, OUT], F32)
        tbT = keep.tile([P, B, 2, P], BF16)
        result = keep.tile([P, B, OUT], F32)

        def quantise_round(first):
            for b in range(first, first + ROUND):
                quantise_rows(
                    nc, psum, stage, ident_f32, x_sb[:, b, :], x_codes[:, b, :], x_scales[:, b, :]
                )

        def multiply_round(first):
            acc = psum.tile([P, ROUND, OUT], F32, tag="bank")
            for i in range(ROUND):
                b = first + i
                for g in range(PASSES):
                    nc.tensor.matmul_mx(
                        out=acc[:, i, :],
                        lhsT=x_codes[:, b, g * S : (g + 1) * S].bitcast(FP8X4),
                        lhsT_scale=x_scales[:, b, g * S : (g + 1) * S],
                        rhs=w_codes[:, g * OUT : (g + 1) * OUT].bitcast(FP8X4),
                        rhs_scale=w_scales[:, g * OUT : (g + 1) * OUT],
                        start=(g == 0),
                        stop=(g == PASSES - 1),
                    )
            nc.vector.tensor_copy(out=base[:, first : first + ROUND, :], in_=acc[:])

        def flip_adapters(first):
            tbT_ps = psum.tile([P, ROUND, 2, P], BF16, tag="bank")
            for i in range(ROUND):
                nc.tensor.transpose(tbT_ps[:, i, 0, :], t_sb[:, first + i, :], ident_bf16[:])
                nc.tensor.transpose(tbT_ps[:, i, 1, :], b_sb[:, first + i, :], ident_bf16[:])
            nc.scalar.copy(out=tbT[:, first : first + ROUND, :, :], in_=tbT_ps[:])

        def add_adapters(first):
            these = slice(first, first + ROUND)
            delta_ps = psum.tile([P, ROUND, OUT], F32, tag="bank")
            for i in range(ROUND):
                nc.tensor.matmul(
                    delta_ps[:, i, :],
                    lhsT=tbT[:, first + i, 0, :],
                    rhs=tbT[:, first + i, 1, :],
                    start=True,
                    stop=True,
                )
            nc.vector.scalar_tensor_tensor(
                out=result[:, these, :],
                in0=delta_ps[:],
                scalar=SCALING,
                in1=base[:, these, :],
                op0=mybir.AluOpType.mult,
                op1=mybir.AluOpType.add,
            )
            nc.sync.dma_start(out=out[these].rearrange("b s o -> s b o"), in_=result[:, these, :])

        with tc.manual_schedule():
            zeros = keep.tile([P, P * PACK], BF16, align_bytes=64)
            nc.vector.memset(zeros[:], 0.0)
            zero_codes = keep.tile([P, P], U32, align_bytes=64)
            zero_scales = keep.tile([P, P], U8, align_bytes=64)
            nc.vector.quantize_mx(
                out=zero_codes[:].bitcast(FP8X4), scales=zero_scales[:], in_=zeros[:]
            )

            def spin():
                warm_ps = psum.tile([P, P], F32, tag="bank")
                for i in range(WARM_PASSES):
                    nc.tensor.matmul_mx(
                        out=warm_ps[:],
                        lhsT=zero_codes[:].bitcast(FP8X4),
                        lhsT_scale=zero_scales[:],
                        rhs=zero_codes[:].bitcast(FP8X4),
                        rhs_scale=zero_scales[:],
                        start=True,
                        stop=True,
                    )

            spin()
            quantise_rows(nc, psum, stage, ident_f32, w_sb[:], w_codes[:], w_scales[:])
            for step in range(2 * ROUNDS + LEAD):
                if step < ROUNDS:
                    quantise_round(step * ROUND)
                elif step < 2 * ROUNDS:
                    flip_adapters((step - ROUNDS) * ROUND)
                due = step - LEAD
                if due < 0:
                    spin()
                elif due < ROUNDS:
                    multiply_round(due * ROUND)
                elif due >= ROUNDS:
                    add_adapters((due - ROUNDS) * ROUND)
